import numpy as np
import ml_dtypes


def mxq(x, axis, fmt="e4m3"):
    dtype, down = {"e4m3": (ml_dtypes.float8_e4m3fn, 7), "e5m2": (ml_dtypes.float8_e5m2, 14)}[fmt]
    v = np.moveaxis(np.asarray(x, np.float32).astype(ml_dtypes.bfloat16).astype(np.float64), axis, -1)
    blocks = v.reshape(v.shape[:-1] + (-1, 32))
    amax = np.abs(blocks).max(-1, keepdims=True)
    byte = np.maximum(np.where(amax > 0, np.frexp(amax)[1] - 1 + 127, 0) - down, 1)
    scale = np.exp2(byte - 127.0)
    codes = (blocks / scale).astype(np.float32).astype(dtype).astype(np.float64)
    return np.moveaxis((codes * scale).reshape(v.shape), -1, axis)


WIDE = False


def mx_kscale(k):
    if not WIDE:
        return np.ones(k)
    levels = np.array([18, -18])
    if k % 512:
        return np.exp2(np.random.permutation(np.resize(levels, k // 32))).repeat(32)
    a = np.empty((k // 512, 16))
    for p in range(k // 512):
        a[p, :8] = np.random.permutation(np.resize(levels, 8))
        for g in range(8):
            far = levels[np.abs(levels - a[p, g]) >= 10]
            a[p, g + 8] = far[np.random.randint(len(far))]
    return np.exp2(a.ravel()).repeat(32)


BF16 = ml_dtypes.bfloat16


def bf(x):
    return np.asarray(x, np.float32).astype(BF16)


def f64(x):
    return np.asarray(x).astype(np.float64)


B, I, J, P = 1024, 512, 512, 8
TEMP = 1.0


def softmax_last(a):
    e = np.exp(a - a.max(-1, keepdims=True))
    return e / e.sum(-1, keepdims=True)


def setup_inputs():
    s = mx_kscale(B)
    r = np.minimum(s, 1.0)[:, None]
    u = mx_kscale(J)
    back = np.ones(P)
    back[6] = np.min(r)
    x0 = bf(np.random.random_sample((B, I)) + 0.5)
    alphas = bf(np.random.standard_normal((I, J, P)))
    coeffs0 = bf(np.random.standard_normal((I, J, P)) * 3.0 / np.sqrt(I))
    gates = softmax_last(f64(alphas) / TEMP)
    g = bf(np.random.standard_normal((B, J)) * np.exp2(np.random.randint(-6, 1, (B, 1))) * r * u)
    return {"x": bf(f64(x0) * r), "alphas": alphas, "coeffs": bf(f64(coeffs0) / u[None, :, None] * back),
            "gates": np.asarray(gates, np.float32), "grad_out": g}


def reference(x, alphas, coeffs, gates, grad_out):
    xf, g = f64(x), f64(grad_out)
    gt = f64(gates)[:, :, 1:]
    ex, inv = np.exp(xf), 1.0 / xf
    p = np.stack([xf, xf * xf, xf * xf * xf, ex, np.log(xf), inv, np.sin(xf)], axis=1)
    d = np.stack([np.ones_like(xf), 2.0 * xf, 3.0 * xf * xf, ex, inv, -inv * inv, np.cos(xf)], axis=1)
    w = (gt * f64(coeffs)[:, :, 1:]).transpose(2, 0, 1).reshape((P - 1) * I, J)
    dp = mxq(g, 1, "e5m2") @ mxq(w, 1, "e4m3").T
    dx = (dp.reshape(B, P - 1, I) * d).sum(1)
    dw = mxq(p.reshape(B, (P - 1) * I), 0, "e4m3").T @ mxq(g, 0, "e5m2")
    dw = dw.reshape(P - 1, I, J).transpose(1, 2, 0)
    dcoeffs = np.concatenate([np.zeros((I, J, 1)), gt * dw], axis=-1)
    return dx, dcoeffs

@@ -1,0 +1,428 @@
+import math
+from contextlib import ExitStack
+
+import concourse.mybir as mybir
+from concourse.masks import make_identity
+
+F32 = mybir.dt.float32
+BF16 = mybir.dt.bfloat16
+U32 = mybir.dt.uint32
+U8 = mybir.dt.uint8
+E4M3 = mybir.dt.float8_e4m3fn_x4
+E5M2 = mybir.dt.float8_e5m2_x4
+ACT = mybir.ActivationFunctionType
+ALU = mybir.AluOpType
+
+TOKENS, IN, OUT, PRIMS = 1024, 512, 512, 8
+FLOPS = 2 * 2 * TOKENS * IN * OUT * (PRIMS - 1)
+BYTES = TOKENS * IN * 2 + IN * OUT * PRIMS * (2 + 4 + 4) + TOKENS * OUT * 2 + TOKENS * IN * 4
+
+P = 128
+PACK = 4
+PASS = P * PACK
+HALVES = TOKENS // PASS
+BLOCKS = IN // P
+STEPS = BLOCKS * HALVES
+LINE = 4
+X, X2, X3, EXP, LN, INV, SIN = 1, 2, 3, 4, 5, 6, 7
+
+
+def tile_dartslayer_v_kernel(tc, x, alphas, coeffs, gates, grad_out, out_0, out_1):
+    nc = tc.nc
+    with ExitStack() as ctx:
+        keep = ctx.enter_context(tc.tile_pool(name="keep", bufs=1))
+        ring = ctx.enter_context(tc.tile_pool(name="ring", bufs=2))
+        shared = ctx.enter_context(tc.tile_pool(name="shared", bufs=1))
+        psum = ctx.enter_context(tc.psum_pool(name="psum", bufs=8))
+        ctx.enter_context(tc.manual_schedule())
+
+        def bank(shape, dtype=F32):
+            return psum.tile(shape, dtype, name="bank")
+
+        def operand(pool, name, width, bufs):
+            codes = pool.tile([P, width], U32, name=name + "_codes", bufs=bufs, align_bytes=64)
+            scales = pool.tile([P, width], U8, name=name + "_scales", bufs=bufs, align_bytes=64)
+            return codes, scales
+
+        def quantize(target, first, count, values, fmt):
+            codes, scales = target
+            cols = slice(first, first + count)
+            nc.vector.quantize_mx(out=codes[:, cols].bitcast(fmt), scales=scales[:, cols], in_=values)
+
+        def by_token(tensor, half):
+            return tensor[half * PASS : (half + 1) * PASS, :].rearrange("(p t) w -> p t w", t=PACK)
+
+        x_raw, g_raw = [], []
+        for source, tiles in ((x, x_raw), (grad_out, g_raw)):
+            for half in range(HALVES):
+                raw = ring.tile([P, PACK, IN], BF16, name="raw_or_deriv", bufs=4)
+                nc.sync.dma_start(out=raw[:], in_=by_token(source, half))
+                tiles.append(raw)
+
+        gate, coeff = {}, {}
+
+        def load_gates(block):
+            gate[block] = ring.tile([P, OUT * PRIMS], F32, name="gate", bufs=3)
+            rows = gates[block * P : (block + 1) * P, :, :]
+            nc.sync.dma_start(out=gate[block][:], in_=rows.rearrange("i j k -> i (j k)"))
+
+        def load_coeffs(block):
+            coeff[block] = ring.tile([P, OUT * PRIMS], BF16, name="coeff")
+            rows = coeffs[block * P : (block + 1) * P, :, :]
+            nc.sync.dma_start(out=coeff[block][:], in_=rows.rearrange("i j k -> i (j k)"))
+
+        for block in range(2):
+            load_gates(block)
+            load_coeffs(block)
+        load_gates(2)
+
+        ident32 = keep.tile([P, P], F32)
+        ident16 = keep.tile([P, P], BF16)
+        make_identity(nc, ident16[:])
+        make_identity(nc, ident32[:])
+
+        def stage(engine_name):
+            first = {"vector": 0, "scalar": 2 * PASS * PACK * 2}[engine_name]
+            return shared.tile([P, PASS * PACK], BF16, name="stage_" + engine_name, bufs=2, offset=first, align_bytes=64)
+
+        def interleaved(flat):
+            return flat.rearrange("p (c n t) -> p c t n", n=4, t=PACK)
+
+        def rows_by_four(rows):
+            return rows.rearrange("p t (c n) -> p c t n", n=4)
+
+        x_int = [keep.tile([P, IN * PACK], BF16, name="x_int%d" % h, align_bytes=64) for h in range(HALVES)]
+        ln_x = [keep.tile([P, PACK, IN], F32, name="ln_x%d" % h) for h in range(HALVES)]
+        x_t = [keep.tile([P, HALVES, PASS], BF16, name="x_t%d" % b) for b in range(BLOCKS)]
+        cos_t = [keep.tile([P, HALVES, PASS], F32, name="cos_t%d" % b) for b in range(BLOCKS)]
+        whole = {(k, h): operand(keep, "prim%d_%d" % (k, h), IN, 1) for k in (X, X2, LN, SIN) for h in range(HALVES)}
+        g_tok = [operand(keep, "g_tok%d" % h, OUT, 1) for h in range(HALVES)]
+        g_feat = [operand(keep, "g_feat%d" % h, PASS, 1) for h in range(HALVES)]
+
+        for half in range(HALVES):
+            nc.scalar.activation(out=ln_x[half][:], in_=x_raw[half][:], func=ACT.Ln)
+            nc.vector.tensor_copy(out=interleaved(x_int[half][:]), in_=rows_by_four(x_raw[half][:]))
+
+        for half in range(HALVES):
+            for block in range(BLOCKS):
+                turned = bank([P, PACK, P], BF16)
+                for t in range(PACK):
+                    nc.tensor.transpose(turned[:, t, :], x_raw[half][:, t, block * P : (block + 1) * P], ident16[:])
+                nc.scalar.copy(out=x_t[block][:, half, :], in_=turned[:].rearrange("i t p -> i (t p)"))
+
+        g_feat_in = []
+        for half in range(HALVES):
+            staged = stage("scalar")
+            staged_words = staged[:].bitcast(F32).rearrange("p (t r u) -> p t r u", t=PACK, u=2)
+            g_words = g_raw[half][:].rearrange("p t j -> p (t j)").bitcast(F32)
+            for pair in range(PACK // 2):
+                turned = bank([P, 2, 2, P])
+                for tt in range(2):
+                    first = (2 * pair + tt) * (OUT // 2)
+                    for u in range(2):
+                        nc.tensor.transpose(turned[:, tt, u, :], g_words[:, first + u : first + OUT // 2 : 2], ident32[:])
+                nc.scalar.copy(
+                    out=staged_words[:, 2 * pair : 2 * pair + 2, :, :], in_=turned[:].rearrange("p t u r -> p t r u")
+                )
+            g_feat_in.append(staged)
+
+        def make_g_tok(half):
+            staged = stage("vector")
+            nc.vector.tensor_copy(out=interleaved(staged[:]), in_=rows_by_four(g_raw[half][:]))
+            return staged
+
+        def make_square(half):
+            staged = stage("vector")
+            nc.vector.tensor_tensor(out=staged[:], in0=x_int[half][:], in1=x_int[half][:], op=ALU.mult)
+            return staged
+
+        def make_ln(half):
+            staged = stage("vector")
+            nc.vector.tensor_copy(out=interleaved(staged[:]), in_=rows_by_four(ln_x[half][:]))
+            return staged
+
+        pending = [(whole[X, half], x_int[half], E4M3) for half in range(HALVES)]
+        for make, targets, fmt in (
+            (make_g_tok, g_tok, E5M2),
+            (make_square, [whole[X2, h] for h in range(HALVES)], E4M3),
+            (make_ln, [whole[LN, h] for h in range(HALVES)], E4M3),
+        ):
+            for half in range(HALVES):
+                target, values, pending_fmt = pending[0]
+                quantize(target, 0, PASS, values[:], pending_fmt)
+                pending = pending[1:] + [(targets[half], make(half), fmt)]
+                if make is make_square:
+                    quantize(g_feat[half], 0, PASS, g_feat_in[half][:], E5M2)
+        for half in range(HALVES):
+            target, values, pending_fmt = pending[half]
+            quantize(target, 0, PASS, values[:], pending_fmt)
+
+        sin_in = []
+        for half in range(HALVES):
+            staged = stage("scalar")
+            nc.scalar.activation(out=staged[:], in_=x_int[half][:], func=ACT.Sin)
+            sin_in.append(staged)
+        for block in range(BLOCKS):
+            nc.scalar.activation(out=cos_t[block][:], in_=x_t[block][:], func=ACT.Sin, scale=-1.0, bias=math.pi / 2)
+
+        w_rows, w_in, w_op = {}, {}, {}
+
+        def w_multiply(part):
+            block, line = divmod(part, 2)
+            w_rows[part] = ring.tile([P, LINE, 2, P, 2], BF16, name="w_rows")
+            gate_view = gate[block][:].rearrange("i (p u e k) -> i p u e k", u=2, e=2, k=PRIMS)
+            coeff_view = coeff[block][:].rearrange("i (p u e k) -> i p u e k", u=2, e=2, k=PRIMS)
+            for pair in range(2):
+                ks = slice(LINE * line + 2 * pair, LINE * line + 2 * pair + 2)
+                for u in range(2):
+                    nc.vector.tensor_tensor(
+                        out=w_rows[part][:, 2 * pair : 2 * pair + 2, u, :, :].rearrange("i k p e -> i p e k"),
+                        in0=gate_view[:, :, u, :, ks],
+                        in1=coeff_view[:, :, u, :, ks],
+                        op=ALU.mult,
+                    )
+            if line == 1 and block + 2 < BLOCKS:
+                load_coeffs(block + 2)
+
+        def w_transpose(part):
+            w_in[part] = ring.tile([P, LINE * P * PACK], BF16, name="w_in", align_bytes=64)
+            in_words = w_in[part][:].bitcast(F32).rearrange("p (k i u) -> p k i u", k=LINE, u=2)
+            row_words = w_rows[part][:].rearrange("i k u p e -> i (k u p e)").bitcast(F32)
+            copies = []
+            for pair in range(2):
+                turned = bank([P, 2, 2, P])
+                first = 1 if (part % 2 == 0 and pair == 0) else 0
+                for kk in range(first, 2):
+                    for u in range(2):
+                        start = ((2 * pair + kk) * 2 + u) * P
+                        nc.tensor.transpose(turned[:, kk, u, :], row_words[:, start : start + P], ident32[:])
+                copies.append(
+                    (
+                        in_words[:, 2 * pair + first : 2 * pair + 2, :, :],
+                        turned[:, first:2, :, :].rearrange("p k u i -> p k i u"),
+                    )
+                )
+            return copies
+
+        def w_copy(copies):
+            for target, source in copies:
+                nc.scalar.copy(out=target, in_=source)
+
+        def w_quantize(part):
+            w_op[part] = operand(ring, "w", LINE * P, 6)
+            spans = ((1, 1), (2, 2)) if part % 2 == 0 else ((0, 4),)
+            for first, count in spans:
+                values = w_in[part][:, first * PASS : (first + count) * PASS]
+                quantize(w_op[part], first * P, count * P, values, E4M3)
+
+        late_in, late = {}, {}
+
+        def late_prims(step):
+            block, line = divmod(step, 2)
+            cols = slice(block * P, (block + 1) * P)
+            for k in ((X3,), (EXP, INV))[line]:
+                staged = ring.tile([P, HALVES, PASS], BF16, name="late_in", bufs=3, align_bytes=64)
+                for half in range(HALVES):
+                    if k == EXP:
+                        source = x_int[half][:, block * PASS : (block + 1) * PASS]
+                        nc.scalar.activation(out=staged[:, half, :], in_=source, func=ACT.Exp)
+                    else:
+                        nc.scalar.activation(
+                            out=interleaved(staged[:, half, :]),
+                            in_=rows_by_four(ln_x[half][:, :, cols]),
+                            func=ACT.Exp,
+                            scale={X3: 3.0, INV: -1.0}[k],
+                        )
+                late_in[k, block] = staged
+
+        def late_quantize(step):
+            block, line = divmod(step, 2)
+            for k in ((X3,), (EXP, INV))[line]:
+                late[k, block] = operand(ring, "late", HALVES * P, 4)
+                values = late_in[k, block][:].rearrange("p g c -> p (g c)")
+                quantize(late[k, block], 0, HALVES * P, values, E4M3)
+
+        def prim_operand(k, block, half):
+            if (k, half) in whole:
+                (codes, scales), first = whole[k, half], block * P
+            else:
+                (codes, scales), first = late[k, block], half * P
+            return codes[:, first : first + P].bitcast(E4M3), scales[:, first : first + P]
+
+        deriv = {}
+
+        def derivs_of_x(step):
+            block, half = divmod(step, 2)
+            pair = ring.tile([P, 2, PASS], F32, name="raw_or_deriv", bufs=4)
+            nc.scalar.activation(out=pair[:, 0, :], in_=x_t[block][:, half, :], func=ACT.Exp)
+            nc.scalar.activation(out=pair[:, 1, :], in_=x_t[block][:, half, :], func=ACT.Square)
+            deriv[step, X2] = (2.0, x_t[block][:, half, :])
+            deriv[step, X3] = (3.0, pair[:, 1, :])
+            deriv[step, EXP] = (1.0, pair[:, 0, :])
+            deriv[step, SIN] = (1.0, cos_t[block][:, half, :])
+
+        def ln_transpose(step):
+            block, half = divmod(step, 2)
+            turned = bank([P, PACK, P])
+            for t in range(PACK):
+                nc.tensor.transpose(turned[:, t, :], ln_x[half][:, t, block * P : (block + 1) * P], ident32[:])
+            return turned
+
+        def derivs_of_ln(step, turned):
+            pair = ring.tile([P, 2, PASS], F32, name="raw_or_deriv", bufs=4)
+            flat = turned[:].rearrange("i t p -> i (t p)")
+            nc.scalar.activation(out=pair[:, 0, :], in_=flat, func=ACT.Exp, scale=-1.0)
+            nc.scalar.activation(out=pair[:, 1, :], in_=flat, func=ACT.Exp, scale=-2.0)
+            deriv[step, LN] = (1.0, pair[:, 0, :])
+            deriv[step, INV] = (-1.0, pair[:, 1, :])
+
+        def dprims(step):
+            block, half = divmod(step, 2)
+            terms = []
+            for k in (X2, SIN, EXP, X3, X, LN, INV):
+                line, slot = divmod(k, LINE)
+                codes, scales = w_op[2 * block + line]
+                cols = slice(slot * P, (slot + 1) * P)
+                product = bank([P, PASS])
+                nc.tensor.matmul_mx(
+                    out=product[:],
+                    lhsT=codes[:, cols].bitcast(E4M3),
+                    lhsT_scale=scales[:, cols],
+                    rhs=g_feat[half][0][:].bitcast(E5M2),
+                    rhs_scale=g_feat[half][1][:],
+                    start=True,
+                    stop=True,
+                )
+                term = ring.tile([P, PASS], F32, name="term", bufs=PRIMS - 1)
+                if k == X:
+                    nc.scalar.copy(out=term[:], in_=product[:])
+                else:
+                    factor, values = deriv[step, k]
+                    nc.vector.scalar_tensor_tensor(
+                        out=term[:], in0=product[:], scalar=factor, in1=values, op0=ALU.mult, op1=ALU.mult
+                    )
+                terms.append(term)
+            return terms
+
+        def sum_terms(terms):
+            total = bank([P, PACK, P])
+            for t in range(PACK):
+                for n, term in enumerate(terms):
+                    nc.tensor.matmul(
+                        out=total[:, t, :],
+                        lhsT=term[:, t * P : (t + 1) * P],
+                        rhs=ident32[:],
+                        is_transpose=True,
+                        start=(n == 0),
+                        stop=(n == len(terms) - 1),
+                    )
+            return total
+
+        def store_dx(step, total):
+            block, half = divmod(step, 2)
+            dx = ring.tile([P, PACK, P], F32, name="dx")
+            nc.scalar.copy(out=dx[:], in_=total[:])
+            nc.sync.dma_start(out=by_token(out_0, half)[:, :, block * P : (block + 1) * P], in_=dx[:])
+
+        def finish_dx(step, terms):
+            block, half = divmod(step, 2)
+            totals = [bank([P, P]) for t in range(PACK)]
+            for n, term in enumerate(terms):
+                for t in range(PACK):
+                    nc.tensor.matmul(
+                        out=totals[t][:],
+                        lhsT=term[:, t * P : (t + 1) * P],
+                        rhs=ident32[:],
+                        is_transpose=True,
+                        start=(n == 0),
+                        stop=(n == len(terms) - 1),
+                    )
+            dx = ring.tile([P, PACK, P], F32, name="dx")
+            for t in range(PACK):
+                if t % 2 == 0:
+                    nc.scalar.copy(out=dx[:, t, :], in_=totals[t][:])
+                else:
+                    nc.vector.tensor_copy(out=dx[:, t, :], in_=totals[t][:])
+            nc.sync.dma_start(out=by_token(out_0, half)[:, :, block * P : (block + 1) * P], in_=dx[:])
+
+        def dw_products(step):
+            block, line = divmod(step, 2)
+            for k in range(max(1, LINE * line), LINE * (line + 1)):
+                product = bank([P, OUT])
+                for half in range(HALVES):
+                    codes, scales = prim_operand(k, block, half)
+                    nc.tensor.matmul_mx(
+                        out=product[:],
+                        lhsT=codes,
+                        lhsT_scale=scales,
+                        rhs=g_tok[half][0][:].bitcast(E5M2),
+                        rhs_scale=g_tok[half][1][:],
+                        start=(half == 0),
+                        stop=(half == HALVES - 1),
+                    )
+                nc.scalar.copy(out=dw[line][:, k % LINE, :], in_=product[:])
+
+        def dw_multiply(step):
+            block, line = divmod(step, 2)
+            gate_view = gate[block][:].rearrange("i (c e l k) -> i c l k e", e=2, l=2, k=LINE)
+            dw_view = dw[line][:].rearrange("i k (c e) -> i c k e", e=2)
+            for side in range(2):
+                pairs = slice(side * OUT // 4, (side + 1) * OUT // 4)
+                target = gate_view[:, pairs, line, :, :]
+                nc.vector.tensor_tensor(out=target, in0=dw_view[:, pairs, :, :], in1=target, op=ALU.mult)
+                if line == 1:
+                    rows = out_1[block * P : (block + 1) * P, :, :].rearrange("i j k -> i (j k)")
+                    cols = slice(side * OUT * PRIMS // 2, (side + 1) * OUT * PRIMS // 2)
+                    nc.sync.dma_start(out=rows[:, cols], in_=gate[block][:, cols])
+            if line == 1 and block + 3 < BLOCKS:
+                load_gates(block + 3)
+
+        w_multiply(0)
+        w_copy(w_transpose(0))
+        w_multiply(1)
+        for half in range(HALVES):
+            quantize(whole[SIN, half], 0, PASS, sin_in[half][:], E4M3)
+        w_copy(w_transpose(1))
+        late_prims(0)
+        late_prims(1)
+        w_quantize(0)
+        w_multiply(2)
+        w_quantize(1)
+        late_quantize(0)
+        derivs_of_x(0)
+        derivs_of_ln(0, ln_transpose(0))
+        w_copy(w_transpose(2))
+        w_multiply(3)
+        late_quantize(1)
+        w_quantize(2)
+
+        dw = [
+            shared.tile([P, LINE, OUT], F32, name="dw%d" % line, offset=line * LINE * OUT * 4, align_bytes=64)
+            for line in range(2)
+        ]
+        nc.gpsimd.memset(dw[0][:, 0, :], 0.0)
+        dw_products(0)
+
+        multiply_at = {0: 4, 1: 5, 3: 6, 4: 7}
+        transpose_at = {0: 3, 1: 4, 2: 5, 4: 6, 5: 7}
+        for step in range(STEPS - 1):
+            terms = dprims(step)
+            if step == 0:
+                dw_multiply(0)
+            derivs_of_x(step + 1)
+            dw_products(step + 1)
+            if step + 2 < STEPS:
+                late_prims(step + 2)
+            derivs_of_ln(step + 1, ln_transpose(step + 1))
+            if step in transpose_at:
+                w_copy(w_transpose(transpose_at[step]))
+            total = sum_terms(terms)
+            if step in multiply_at:
+                w_multiply(multiply_at[step])
+            dw_multiply(step + 1)
+            store_dx(step, total)
+            if step in transpose_at:
+                w_quantize(transpose_at[step])
+            if step + 2 < STEPS:
+                late_quantize(step + 2)
+        finish_dx(STEPS - 1, dprims(STEPS - 1))

@@ -25,6 +25,8 @@ BLOCKS = IN // P
 STEPS = BLOCKS * HALVES
 LINE = 4
 X, X2, X3, EXP, LN, INV, SIN = 1, 2, 3, 4, 5, 6, 7
+EARLY_DW = ((X, X2), (LN, SIN, EXP))
+LAST_DW = ((X3,), (INV,))
 
 
 def tile_dartslayer_v_kernel(tc, x, alphas, coeffs, gates, grad_out, out_0, out_1):
@@ -209,7 +211,7 @@ def tile_dartslayer_v_kernel(tc, x, alphas, coeffs, gates, grad_out, out_0, out_
                 nc.scalar.copy(out=target, in_=source)
 
         def w_quantize(part):
-            w_op[part] = operand(ring, "w", LINE * P, 6)
+            w_op[part] = operand(ring, "w", LINE * P, 4)
             spans = ((1, 1), (2, 2)) if part % 2 == 0 else ((0, 4),)
             for first, count in spans:
                 values = w_in[part][:, first * PASS : (first + count) * PASS]
@@ -217,28 +219,30 @@ def tile_dartslayer_v_kernel(tc, x, alphas, coeffs, gates, grad_out, out_0, out_
 
         late_in, late = {}, {}
 
-        def late_prims(step):
+        def late_list(step):
             block, line = divmod(step, 2)
-            cols = slice(block * P, (block + 1) * P)
-            for k in ((X3,), (EXP, INV))[line]:
-                staged = ring.tile([P, HALVES, PASS], BF16, name="late_in", bufs=3, align_bytes=64)
+            if line == 1:
+                return [(k, block + 1) for k in (X3, EXP)]
+            return [(INV, block)]
+
+        def late_prims(wanted):
+            for k, block in wanted:
+                staged = ring.tile([P, HALVES, PASS], BF16, name="late_in", bufs=4, align_bytes=64)
                 for half in range(HALVES):
-                    if k == EXP:
-                        source = x_int[half][:, block * PASS : (block + 1) * PASS]
-                        nc.scalar.activation(out=staged[:, half, :], in_=source, func=ACT.Exp)
+                    from_x = x_int[half][:, block * PASS : (block + 1) * PASS]
+                    from_ln = rows_by_four(ln_x[half][:, :, block * P : (block + 1) * P])
+                    if k == EXP or k == X2:
+                        nc.scalar.activation(out=staged[:, half, :], in_=from_x, func={EXP: ACT.Exp, X2: ACT.Square}[k])
+                    elif k == LN:
+                        nc.scalar.copy(out=interleaved(staged[:, half, :]), in_=from_ln)
                     else:
-                        nc.scalar.activation(
-                            out=interleaved(staged[:, half, :]),
-                            in_=rows_by_four(ln_x[half][:, :, cols]),
-                            func=ACT.Exp,
-                            scale={X3: 3.0, INV: -1.0}[k],
-                        )
+                        scale = {X3: 3.0, INV: -1.0}[k]
+                        nc.scalar.activation(out=interleaved(staged[:, half, :]), in_=from_ln, func=ACT.Exp, scale=scale)
                 late_in[k, block] = staged
 
-        def late_quantize(step):
-            block, line = divmod(step, 2)
-            for k in ((X3,), (EXP, INV))[line]:
-                late[k, block] = operand(ring, "late", HALVES * P, 4)
+        def late_quantize(wanted):
+            for k, block in wanted:
+                late[k, block] = operand(ring, "late", HALVES * P, 6)
                 values = late_in[k, block][:].rearrange("p g c -> p (g c)")
                 quantize(late[k, block], 0, HALVES * P, values, E4M3)
 
@@ -279,7 +283,7 @@ def tile_dartslayer_v_kernel(tc, x, alphas, coeffs, gates, grad_out, out_0, out_
         def dprims(step):
             block, half = divmod(step, 2)
             terms = []
-            for k in (X2, SIN, EXP, X3, X, LN, INV):
+            for k in (X2, SIN, EXP, X3, LN, INV, X):
                 line, slot = divmod(k, LINE)
                 codes, scales = w_op[2 * block + line]
                 cols = slice(slot * P, (slot + 1) * P)
@@ -293,16 +297,16 @@ def tile_dartslayer_v_kernel(tc, x, alphas, coeffs, gates, grad_out, out_0, out_
                     start=True,
                     stop=True,
                 )
-                term = ring.tile([P, PASS], F32, name="term", bufs=PRIMS - 1)
                 if k == X:
-                    nc.scalar.copy(out=term[:], in_=product[:])
+                    nc.vector.tensor_tensor(out=terms[0][:], in0=product[:], in1=terms[0][:], op=ALU.add)
                 else:
+                    term = ring.tile([P, PASS], F32, name="term", bufs=PRIMS - 2)
                     factor, values = deriv[step, k]
                     nc.vector.scalar_tensor_tensor(
                         out=term[:], in0=product[:], scalar=factor, in1=values, op0=ALU.mult, op1=ALU.mult
                     )
-                terms.append(term)
-            return terms
+                    terms.append(term)
+            return terms[1:] + terms[:1]
 
         def sum_terms(terms):
             total = bank([P, PACK, P])
@@ -345,9 +349,9 @@ def tile_dartslayer_v_kernel(tc, x, alphas, coeffs, gates, grad_out, out_0, out_
                     nc.vector.tensor_copy(out=dx[:, t, :], in_=totals[t][:])
             nc.sync.dma_start(out=by_token(out_0, half)[:, :, block * P : (block + 1) * P], in_=dx[:])
 
-        def dw_products(step):
+        def dw_products(step, prims, copy):
             block, line = divmod(step, 2)
-            for k in range(max(1, LINE * line), LINE * (line + 1)):
+            for k in prims[line]:
                 product = bank([P, OUT])
                 for half in range(HALVES):
                     codes, scales = prim_operand(k, block, half)
@@ -360,69 +364,63 @@ def tile_dartslayer_v_kernel(tc, x, alphas, coeffs, gates, grad_out, out_0, out_
                         start=(half == 0),
                         stop=(half == HALVES - 1),
                     )
-                nc.scalar.copy(out=dw[line][:, k % LINE, :], in_=product[:])
+                copy(out=dw[line][:, k % LINE, :], in_=product[:])
 
         def dw_multiply(step):
             block, line = divmod(step, 2)
-            gate_view = gate[block][:].rearrange("i (c e l k) -> i c l k e", e=2, l=2, k=LINE)
-            dw_view = dw[line][:].rearrange("i k (c e) -> i c k e", e=2)
-            for side in range(2):
-                pairs = slice(side * OUT // 4, (side + 1) * OUT // 4)
-                target = gate_view[:, pairs, line, :, :]
-                nc.vector.tensor_tensor(out=target, in0=dw_view[:, pairs, :, :], in1=target, op=ALU.mult)
+            gate_view = gate[block][:].rearrange("i (j l k) -> i j l k", l=2, k=LINE)
+            dw_view = dw[line][:].rearrange("i k j -> i j k")
+            sides = 4 if step + 1 == STEPS else 2
+            for side in range(sides):
+                outs = slice(side * OUT // sides, (side + 1) * OUT // sides)
+                target = gate_view[:, outs, line, :]
+                nc.gpsimd.tensor_tensor(out=target, in0=dw_view[:, outs, :], in1=target, op=ALU.mult)
                 if line == 1:
                     rows = out_1[block * P : (block + 1) * P, :, :].rearrange("i j k -> i (j k)")
-                    cols = slice(side * OUT * PRIMS // 2, (side + 1) * OUT * PRIMS // 2)
+                    cols = slice(outs.start * PRIMS, outs.stop * PRIMS)
                     nc.sync.dma_start(out=rows[:, cols], in_=gate[block][:, cols])
             if line == 1 and block + 3 < BLOCKS:
                 load_gates(block + 3)
-
-        w_multiply(0)
-        w_copy(w_transpose(0))
-        w_multiply(1)
-        for half in range(HALVES):
-            quantize(whole[SIN, half], 0, PASS, sin_in[half][:], E4M3)
-        w_copy(w_transpose(1))
-        late_prims(0)
-        late_prims(1)
-        w_quantize(0)
-        w_multiply(2)
-        w_quantize(1)
-        late_quantize(0)
-        derivs_of_x(0)
-        derivs_of_ln(0, ln_transpose(0))
-        w_copy(w_transpose(2))
-        w_multiply(3)
-        late_quantize(1)
-        w_quantize(2)
 
         dw = [
             shared.tile([P, LINE, OUT], F32, name="dw%d" % line, offset=line * LINE * OUT * 4, align_bytes=64)
             for line in range(2)
         ]
         nc.gpsimd.memset(dw[0][:, 0, :], 0.0)
-        dw_products(0)
+        dw_products(0, EARLY_DW, nc.scalar.copy)
+        w_multiply(0)
+        w_copy(w_transpose(0))
+        w_multiply(1)
+        for half in range(HALVES):
+            quantize(whole[SIN, half], 0, PASS, sin_in[half][:], E4M3)
+        w_copy(w_transpose(1))
+        late_prims([(X3, 0)])
+        w_quantize(0)
+        w_multiply(2)
+        w_quantize(1)
+        late_quantize([(X3, 0)])
+        derivs_of_x(0)
+        derivs_of_ln(0, ln_transpose(0))
+        late_prims([(EXP, 0)])
 
-        multiply_at = {0: 4, 1: 5, 3: 6, 4: 7}
-        transpose_at = {0: 3, 1: 4, 2: 5, 4: 6, 5: 7}
-        for step in range(STEPS - 1):
+        for step in range(STEPS):
+            dw_products(step, LAST_DW, nc.vector.tensor_copy)
+            dw_multiply(step)
             terms = dprims(step)
             if step == 0:
-                dw_multiply(0)
+                late_quantize([(EXP, 0)])
+            if step + 1 == STEPS:
+                finish_dx(step, terms)
+                continue
+            late_prims(late_list(step))
             derivs_of_x(step + 1)
-            dw_products(step + 1)
-            if step + 2 < STEPS:
-                late_prims(step + 2)
+            dw_products(step + 1, EARLY_DW, nc.scalar.copy)
             derivs_of_ln(step + 1, ln_transpose(step + 1))
-            if step in transpose_at:
-                w_copy(w_transpose(transpose_at[step]))
-            total = sum_terms(terms)
-            if step in multiply_at:
-                w_multiply(multiply_at[step])
-            dw_multiply(step + 1)
-            store_dx(step, total)
-            if step in transpose_at:
-                w_quantize(transpose_at[step])
             if step + 2 < STEPS:
-                late_quantize(step + 2)
-        finish_dx(STEPS - 1, dprims(STEPS - 1))
+                w_copy(w_transpose(step + 2))
+            store_dx(step, sum_terms(terms))
+            late_quantize(late_list(step))
+            if step + 3 < STEPS:
+                w_multiply(step + 3)
+            if step + 2 < STEPS:
+                w_quantize(step + 2)

@@ -26,7 +26,8 @@ STEPS = BLOCKS * HALVES
 LINE = 4
 X, X2, X3, EXP, LN, INV, SIN = 1, 2, 3, 4, 5, 6, 7
 EARLY_DW = ((X, X2), (LN, SIN, EXP))
-LAST_DW = ((X3,), (INV,))
+GPSIMD_OUTS = 256
+LAST_DW = (X3, INV)
 
 
 def tile_dartslayer_v_kernel(tc, x, alphas, coeffs, gates, grad_out, out_0, out_1):
@@ -221,9 +222,9 @@ def tile_dartslayer_v_kernel(tc, x, alphas, coeffs, gates, grad_out, out_0, out_
 
         def late_list(step):
             block, line = divmod(step, 2)
-            if line == 1:
-                return [(k, block + 1) for k in (X3, EXP)]
-            return [(INV, block)]
+            if block + 1 == BLOCKS:
+                return []
+            return [(k, block + 1) for k in ((X3,), (EXP, INV))[line]]
 
         def late_prims(wanted):
             for k, block in wanted:
@@ -283,7 +284,7 @@ def tile_dartslayer_v_kernel(tc, x, alphas, coeffs, gates, grad_out, out_0, out_
         def dprims(step):
             block, half = divmod(step, 2)
             terms = []
-            for k in (X2, SIN, EXP, X3, LN, INV, X):
+            for k in (X2, X, SIN, EXP, X3, LN, INV):
                 line, slot = divmod(k, LINE)
                 codes, scales = w_op[2 * block + line]
                 cols = slice(slot * P, (slot + 1) * P)
@@ -298,15 +299,17 @@ def tile_dartslayer_v_kernel(tc, x, alphas, coeffs, gates, grad_out, out_0, out_
                     stop=True,
                 )
                 if k == X:
-                    nc.vector.tensor_tensor(out=terms[0][:], in0=product[:], in1=terms[0][:], op=ALU.add)
+                    term = ring.tile([P, PASS], F32, name="term", bufs=PRIMS - 1)
+                    nc.scalar.copy(out=term[:], in_=product[:])
+                    terms.append(term)
                 else:
-                    term = ring.tile([P, PASS], F32, name="term", bufs=PRIMS - 2)
+                    term = ring.tile([P, PASS], F32, name="term", bufs=PRIMS - 1)
                     factor, values = deriv[step, k]
                     nc.vector.scalar_tensor_tensor(
-                        out=term[:], in0=product[:], scalar=factor, in1=values, op0=ALU.mult, op1=ALU.mult
+                        out=term[:], in0=values, scalar=factor, in1=product[:], op0=ALU.mult, op1=ALU.mult
                     )
                     terms.append(term)
-            return terms[1:] + terms[:1]
+            return terms
 
         def sum_terms(terms):
             total = bank([P, PACK, P])
@@ -349,36 +352,57 @@ def tile_dartslayer_v_kernel(tc, x, alphas, coeffs, gates, grad_out, out_0, out_
                     nc.vector.tensor_copy(out=dx[:, t, :], in_=totals[t][:])
             nc.sync.dma_start(out=by_token(out_0, half)[:, :, block * P : (block + 1) * P], in_=dx[:])
 
-        def dw_products(step, prims, copy):
-            block, line = divmod(step, 2)
-            for k in prims[line]:
-                product = bank([P, OUT])
-                for half in range(HALVES):
-                    codes, scales = prim_operand(k, block, half)
-                    nc.tensor.matmul_mx(
-                        out=product[:],
-                        lhsT=codes,
-                        lhsT_scale=scales,
-                        rhs=g_tok[half][0][:].bitcast(E5M2),
-                        rhs_scale=g_tok[half][1][:],
-                        start=(half == 0),
-                        stop=(half == HALVES - 1),
-                    )
-                copy(out=dw[line][:, k % LINE, :], in_=product[:])
+        def dw_product(step, k):
+            block = step // 2
+            product = bank([P, OUT])
+            for half in range(HALVES):
+                codes, scales = prim_operand(k, block, half)
+                nc.tensor.matmul_mx(
+                    out=product[:],
+                    lhsT=codes,
+                    lhsT_scale=scales,
+                    rhs=g_tok[half][0][:].bitcast(E5M2),
+                    rhs_scale=g_tok[half][1][:],
+                    start=(half == 0),
+                    stop=(half == HALVES - 1),
+                )
+            return product
 
-        def dw_multiply(step):
+        def dw_products(step):
+            line = step % 2
+            for k in EARLY_DW[line]:
+                nc.scalar.copy(out=dw[line][:, k % LINE, :], in_=dw_product(step, k)[:])
+            return dw_product(step, LAST_DW[line])
+
+        def dw_last_copy(step, product, outs):
+            line = step % 2
+            nc.vector.tensor_copy(out=dw[line][:, LAST_DW[line] % LINE, outs], in_=product[:, outs])
+
+        def store_dw(step, outs):
+            block, line = divmod(step, 2)
+            if line == 1:
+                rows = out_1[block * P : (block + 1) * P, :, :].rearrange("i j k -> i (j k)")
+                cols = slice(outs.start * PRIMS, outs.stop * PRIMS)
+                nc.sync.dma_start(out=rows[:, cols], in_=gate[block][:, cols])
+
+        def dw_multiply_gpsimd(step):
             block, line = divmod(step, 2)
             gate_view = gate[block][:].rearrange("i (j l k) -> i j l k", l=2, k=LINE)
             dw_view = dw[line][:].rearrange("i k j -> i j k")
-            sides = 4 if step + 1 == STEPS else 2
-            for side in range(sides):
-                outs = slice(side * OUT // sides, (side + 1) * OUT // sides)
+            for first in range(0, GPSIMD_OUTS, GPSIMD_OUTS // 2):
+                outs = slice(first, first + GPSIMD_OUTS // 2)
                 target = gate_view[:, outs, line, :]
                 nc.gpsimd.tensor_tensor(out=target, in0=dw_view[:, outs, :], in1=target, op=ALU.mult)
-                if line == 1:
-                    rows = out_1[block * P : (block + 1) * P, :, :].rearrange("i j k -> i (j k)")
-                    cols = slice(outs.start * PRIMS, outs.stop * PRIMS)
-                    nc.sync.dma_start(out=rows[:, cols], in_=gate[block][:, cols])
+                store_dw(step, outs)
+
+        def dw_multiply_vector(step):
+            block, line = divmod(step, 2)
+            gate_view = gate[block][:].rearrange("i (c e l k) -> i c l k e", e=2, l=2, k=LINE)
+            dw_view = dw[line][:].rearrange("i k (c e) -> i c k e", e=2)
+            pairs = slice(GPSIMD_OUTS // 2, OUT // 2)
+            target = gate_view[:, pairs, line, :, :]
+            nc.vector.tensor_tensor(out=target, in0=dw_view[:, pairs, :, :], in1=target, op=ALU.mult)
+            store_dw(step, slice(GPSIMD_OUTS, OUT))
             if line == 1 and block + 3 < BLOCKS:
                 load_gates(block + 3)
 
@@ -387,34 +411,32 @@ def tile_dartslayer_v_kernel(tc, x, alphas, coeffs, gates, grad_out, out_0, out_
             for line in range(2)
         ]
         nc.gpsimd.memset(dw[0][:, 0, :], 0.0)
-        dw_products(0, EARLY_DW, nc.scalar.copy)
         w_multiply(0)
         w_copy(w_transpose(0))
         w_multiply(1)
         for half in range(HALVES):
             quantize(whole[SIN, half], 0, PASS, sin_in[half][:], E4M3)
         w_copy(w_transpose(1))
-        late_prims([(X3, 0)])
+        late_prims(late_list(-2))
         w_quantize(0)
         w_multiply(2)
         w_quantize(1)
-        late_quantize([(X3, 0)])
+        late_quantize(late_list(-2))
+        held = dw_products(0)
         derivs_of_x(0)
         derivs_of_ln(0, ln_transpose(0))
-        late_prims([(EXP, 0)])
+        late_prims(late_list(-1))
 
-        for step in range(STEPS):
-            dw_products(step, LAST_DW, nc.vector.tensor_copy)
-            dw_multiply(step)
+        for step in range(STEPS - 1):
+            dw_last_copy(step, held, slice(0, OUT))
+            dw_multiply_gpsimd(step)
             terms = dprims(step)
             if step == 0:
-                late_quantize([(EXP, 0)])
-            if step + 1 == STEPS:
-                finish_dx(step, terms)
-                continue
+                late_quantize(late_list(-1))
+            dw_multiply_vector(step)
             late_prims(late_list(step))
             derivs_of_x(step + 1)
-            dw_products(step + 1, EARLY_DW, nc.scalar.copy)
+            held = dw_products(step + 1)
             derivs_of_ln(step + 1, ln_transpose(step + 1))
             if step + 2 < STEPS:
                 w_copy(w_transpose(step + 2))
@@ -424,3 +446,9 @@ def tile_dartslayer_v_kernel(tc, x, alphas, coeffs, gates, grad_out, out_0, out_
                 w_multiply(step + 3)
             if step + 2 < STEPS:
                 w_quantize(step + 2)
+        step = STEPS - 1
+        dw_last_copy(step, held, slice(GPSIMD_OUTS, OUT))
+        dw_multiply_vector(step)
+        dw_last_copy(step, held, slice(0, GPSIMD_OUTS))
+        dw_multiply_gpsimd(step)
+        finish_dx(step, dprims(step))

@@ -22,12 +22,25 @@ PACK = 4
 PASS = P * PACK
 HALVES = TOKENS // PASS
 BLOCKS = IN // P
-STEPS = BLOCKS * HALVES
-LINE = 4
+QUAD = 4
+STEPS = BLOCKS * 2
+MX_ALIGN = 64
 X, X2, X3, EXP, LN, INV, SIN = 1, 2, 3, 4, 5, 6, 7
+
+WHOLE_PRIMS = (X, X2, LN, SIN)
+EXP_PRIMS = ((X3,), (EXP, INV))
 EARLY_DW = ((X, X2), (LN, SIN, EXP))
-GPSIMD_OUTS = 256
 LAST_DW = (X3, INV)
+
+GPSIMD_OUTS = 256
+HELD_OUTS = 64
+W_AHEAD = 3
+
+GATE_BUFS = 3
+RAW_OR_DERIV_BUFS = 4
+W_BUFS = 4
+EXP_IN_BUFS = 4
+EXP_OPERAND_BUFS = 6
 
 
 def tile_dartslayer_v_kernel(tc, x, alphas, coeffs, gates, grad_out, out_0, out_1):
@@ -43,8 +56,8 @@ def tile_dartslayer_v_kernel(tc, x, alphas, coeffs, gates, grad_out, out_0, out_
             return psum.tile(shape, dtype, name="bank")
 
         def operand(pool, name, width, bufs):
-            codes = pool.tile([P, width], U32, name=name + "_codes", bufs=bufs, align_bytes=64)
-            scales = pool.tile([P, width], U8, name=name + "_scales", bufs=bufs, align_bytes=64)
+            codes = pool.tile([P, width], U32, name=name + "_codes", bufs=bufs, align_bytes=MX_ALIGN)
+            scales = pool.tile([P, width], U8, name=name + "_scales", bufs=bufs, align_bytes=MX_ALIGN)
             return codes, scales
 
         def quantize(target, first, count, values, fmt):
@@ -58,14 +71,14 @@ def tile_dartslayer_v_kernel(tc, x, alphas, coeffs, gates, grad_out, out_0, out_
         x_raw, g_raw = [], []
         for source, tiles in ((x, x_raw), (grad_out, g_raw)):
             for half in range(HALVES):
-                raw = ring.tile([P, PACK, IN], BF16, name="raw_or_deriv", bufs=4)
+                raw = ring.tile([P, PACK, IN], BF16, name="raw_or_deriv", bufs=RAW_OR_DERIV_BUFS)
                 nc.sync.dma_start(out=raw[:], in_=by_token(source, half))
                 tiles.append(raw)
 
         gate, coeff = {}, {}
 
         def load_gates(block):
-            gate[block] = ring.tile([P, OUT * PRIMS], F32, name="gate", bufs=3)
+            gate[block] = ring.tile([P, OUT * PRIMS], F32, name="gate", bufs=GATE_BUFS)
             rows = gates[block * P : (block + 1) * P, :, :]
             nc.sync.dma_start(out=gate[block][:], in_=rows.rearrange("i j k -> i (j k)"))
 
@@ -84,9 +97,10 @@ def tile_dartslayer_v_kernel(tc, x, alphas, coeffs, gates, grad_out, out_0, out_
         make_identity(nc, ident16[:])
         make_identity(nc, ident32[:])
 
-        def stage(engine_name):
-            first = {"vector": 0, "scalar": 2 * PASS * PACK * 2}[engine_name]
-            return shared.tile([P, PASS * PACK], BF16, name="stage_" + engine_name, bufs=2, offset=first, align_bytes=64)
+        def stage(ring_index):
+            offset = ring_index * 2 * PASS * PACK * 2
+            name = "stage%d" % ring_index
+            return shared.tile([P, PASS * PACK], BF16, name=name, bufs=2, offset=offset, align_bytes=MX_ALIGN)
 
         def interleaved(flat):
             return flat.rearrange("p (c n t) -> p c t n", n=4, t=PACK)
@@ -94,11 +108,11 @@ def tile_dartslayer_v_kernel(tc, x, alphas, coeffs, gates, grad_out, out_0, out_
         def rows_by_four(rows):
             return rows.rearrange("p t (c n) -> p c t n", n=4)
 
-        x_int = [keep.tile([P, IN * PACK], BF16, name="x_int%d" % h, align_bytes=64) for h in range(HALVES)]
+        x_int = [keep.tile([P, IN * PACK], BF16, name="x_int%d" % h, align_bytes=MX_ALIGN) for h in range(HALVES)]
         ln_x = [keep.tile([P, PACK, IN], F32, name="ln_x%d" % h) for h in range(HALVES)]
         x_t = [keep.tile([P, HALVES, PASS], BF16, name="x_t%d" % b) for b in range(BLOCKS)]
         cos_t = [keep.tile([P, HALVES, PASS], F32, name="cos_t%d" % b) for b in range(BLOCKS)]
-        whole = {(k, h): operand(keep, "prim%d_%d" % (k, h), IN, 1) for k in (X, X2, LN, SIN) for h in range(HALVES)}
+        whole = {(k, h): operand(keep, "prim%d_%d" % (k, h), IN, 1) for k in WHOLE_PRIMS for h in range(HALVES)}
         g_tok = [operand(keep, "g_tok%d" % h, OUT, 1) for h in range(HALVES)]
         g_feat = [operand(keep, "g_feat%d" % h, PASS, 1) for h in range(HALVES)]
 
@@ -113,152 +127,155 @@ def tile_dartslayer_v_kernel(tc, x, alphas, coeffs, gates, grad_out, out_0, out_
                     nc.tensor.transpose(turned[:, t, :], x_raw[half][:, t, block * P : (block + 1) * P], ident16[:])
                 nc.scalar.copy(out=x_t[block][:, half, :], in_=turned[:].rearrange("i t p -> i (t p)"))
 
-        g_feat_in = []
-        for half in range(HALVES):
-            staged = stage("scalar")
+        def g_transpose(half):
+            staged = stage(1)
             staged_words = staged[:].bitcast(F32).rearrange("p (t r u) -> p t r u", t=PACK, u=2)
             g_words = g_raw[half][:].rearrange("p t j -> p (t j)").bitcast(F32)
-            for pair in range(PACK // 2):
+            copies = []
+            for slot_pair in range(PACK // 2):
                 turned = bank([P, 2, 2, P])
                 for tt in range(2):
-                    first = (2 * pair + tt) * (OUT // 2)
+                    first = (2 * slot_pair + tt) * (OUT // 2)
                     for u in range(2):
                         nc.tensor.transpose(turned[:, tt, u, :], g_words[:, first + u : first + OUT // 2 : 2], ident32[:])
-                nc.scalar.copy(
-                    out=staged_words[:, 2 * pair : 2 * pair + 2, :, :], in_=turned[:].rearrange("p t u r -> p t r u")
-                )
-            g_feat_in.append(staged)
+                target = staged_words[:, 2 * slot_pair : 2 * slot_pair + 2, :, :]
+                copies.append((target, turned[:].rearrange("p t u r -> p t r u")))
+            return staged, copies
 
-        def make_g_tok(half):
-            staged = stage("vector")
-            nc.vector.tensor_copy(out=interleaved(staged[:]), in_=rows_by_four(g_raw[half][:]))
+        def copy_all(copy, copies):
+            for target, source in copies:
+                copy(out=target, in_=source)
+
+        g_feat_in, g_copies = zip(*[g_transpose(half) for half in range(HALVES)])
+        copy_all(nc.scalar.copy, g_copies[0])
+
+        def interleave(rows):
+            staged = stage(0)
+            nc.vector.tensor_copy(out=interleaved(staged[:]), in_=rows_by_four(rows))
             return staged
 
-        def make_square(half):
-            staged = stage("vector")
-            nc.vector.tensor_tensor(out=staged[:], in0=x_int[half][:], in1=x_int[half][:], op=ALU.mult)
-            return staged
-
-        def make_ln(half):
-            staged = stage("vector")
-            nc.vector.tensor_copy(out=interleaved(staged[:]), in_=rows_by_four(ln_x[half][:]))
-            return staged
-
-        pending = [(whole[X, half], x_int[half], E4M3) for half in range(HALVES)]
-        for make, targets, fmt in (
-            (make_g_tok, g_tok, E5M2),
-            (make_square, [whole[X2, h] for h in range(HALVES)], E4M3),
-            (make_ln, [whole[LN, h] for h in range(HALVES)], E4M3),
-        ):
-            for half in range(HALVES):
-                target, values, pending_fmt = pending[0]
-                quantize(target, 0, PASS, values[:], pending_fmt)
-                pending = pending[1:] + [(targets[half], make(half), fmt)]
-                if make is make_square:
-                    quantize(g_feat[half], 0, PASS, g_feat_in[half][:], E5M2)
+        g_tok_in = []
         for half in range(HALVES):
-            target, values, pending_fmt = pending[half]
-            quantize(target, 0, PASS, values[:], pending_fmt)
+            quantize(whole[X, half], 0, IN, x_int[half][:], E4M3)
+            g_tok_in.append(interleave(g_raw[half][:]))
+        copy_all(nc.vector.tensor_copy, g_copies[1])
+        for half in range(HALVES):
+            quantize(g_tok[half], 0, OUT, g_tok_in[half][:], E5M2)
+            quantize(g_feat[half], 0, PASS, g_feat_in[half][:], E5M2)
 
         sin_in = []
         for half in range(HALVES):
-            staged = stage("scalar")
+            staged = stage(1)
             nc.scalar.activation(out=staged[:], in_=x_int[half][:], func=ACT.Sin)
             sin_in.append(staged)
-        for block in range(BLOCKS):
-            nc.scalar.activation(out=cos_t[block][:], in_=x_t[block][:], func=ACT.Sin, scale=-1.0, bias=math.pi / 2)
+
+        def cosines(blocks):
+            for block in blocks:
+                nc.scalar.activation(out=cos_t[block][:], in_=x_t[block][:], func=ACT.Sin, scale=-1.0, bias=math.pi / 2)
+
+        def finish_whole_prims():
+            squares, logs = [], []
+            for half in range(HALVES):
+                staged = stage(0)
+                nc.vector.tensor_tensor(out=staged[:], in0=x_int[half][:], in1=x_int[half][:], op=ALU.mult)
+                squares.append(staged)
+            for half in range(HALVES):
+                quantize(whole[X2, half], 0, IN, squares[half][:], E4M3)
+                logs.append(interleave(ln_x[half][:]))
+            for half in range(HALVES):
+                quantize(whole[SIN, half], 0, IN, sin_in[half][:], E4M3)
+                quantize(whole[LN, half], 0, IN, logs[half][:], E4M3)
 
         w_rows, w_in, w_op = {}, {}, {}
 
+        def first_slot(part):
+            return 1 if part % 2 == 0 else 0
+
         def w_multiply(part):
-            block, line = divmod(part, 2)
-            w_rows[part] = ring.tile([P, LINE, 2, P, 2], BF16, name="w_rows")
-            gate_view = gate[block][:].rearrange("i (p u e k) -> i p u e k", u=2, e=2, k=PRIMS)
-            coeff_view = coeff[block][:].rearrange("i (p u e k) -> i p u e k", u=2, e=2, k=PRIMS)
-            for pair in range(2):
-                ks = slice(LINE * line + 2 * pair, LINE * line + 2 * pair + 2)
+            block, quad = divmod(part, 2)
+            w_rows[part] = ring.tile([P, QUAD, 2, P, 2], BF16, name="w_rows")
+            gate_view = gate[block][:].rearrange("i (p u e k) -> i u p e k", u=2, e=2, k=PRIMS)
+            coeff_view = coeff[block][:].rearrange("i (p u e k) -> i u p e k", u=2, e=2, k=PRIMS)
+            if quad == 0:
+                nc.vector.tensor_tensor(
+                    out=w_rows[part][:, X, :, :, :],
+                    in0=gate_view[:, :, :, :, X],
+                    in1=coeff_view[:, :, :, :, X],
+                    op=ALU.mult,
+                )
+            for slot in range(2 * first_slot(part), QUAD, 2):
+                ks = slice(QUAD * quad + slot, QUAD * quad + slot + 2)
                 for u in range(2):
                     nc.vector.tensor_tensor(
-                        out=w_rows[part][:, 2 * pair : 2 * pair + 2, u, :, :].rearrange("i k p e -> i p e k"),
-                        in0=gate_view[:, :, u, :, ks],
-                        in1=coeff_view[:, :, u, :, ks],
+                        out=w_rows[part][:, slot : slot + 2, u, :, :].rearrange("i k p e -> i p e k"),
+                        in0=gate_view[:, u, :, :, ks],
+                        in1=coeff_view[:, u, :, :, ks],
                         op=ALU.mult,
                     )
-            if line == 1 and block + 2 < BLOCKS:
+            if quad == 1 and block + 2 < BLOCKS:
                 load_coeffs(block + 2)
 
         def w_transpose(part):
-            w_in[part] = ring.tile([P, LINE * P * PACK], BF16, name="w_in", align_bytes=64)
-            in_words = w_in[part][:].bitcast(F32).rearrange("p (k i u) -> p k i u", k=LINE, u=2)
+            w_in[part] = ring.tile([P, QUAD * P * PACK], BF16, name="w_in", align_bytes=MX_ALIGN)
+            in_words = w_in[part][:].bitcast(F32).rearrange("p (k i u) -> p k i u", k=QUAD, u=2)
             row_words = w_rows[part][:].rearrange("i k u p e -> i (k u p e)").bitcast(F32)
             copies = []
-            for pair in range(2):
+            for slot in range(0, QUAD, 2):
                 turned = bank([P, 2, 2, P])
-                first = 1 if (part % 2 == 0 and pair == 0) else 0
-                for kk in range(first, 2):
+                skip = max(first_slot(part) - slot, 0)
+                for kk in range(skip, 2):
                     for u in range(2):
-                        start = ((2 * pair + kk) * 2 + u) * P
-                        nc.tensor.transpose(turned[:, kk, u, :], row_words[:, start : start + P], ident32[:])
-                copies.append(
-                    (
-                        in_words[:, 2 * pair + first : 2 * pair + 2, :, :],
-                        turned[:, first:2, :, :].rearrange("p k u i -> p k i u"),
-                    )
-                )
-            return copies
-
-        def w_copy(copies):
-            for target, source in copies:
-                nc.scalar.copy(out=target, in_=source)
+                        first = ((slot + kk) * 2 + u) * P
+                        nc.tensor.transpose(turned[:, kk, u, :], row_words[:, first : first + P], ident32[:])
+                source = turned[:, skip:2, :, :].rearrange("p k u i -> p k i u")
+                copies.append((in_words[:, slot + skip : slot + 2, :, :], source))
+            copy_all(nc.scalar.copy, copies)
 
         def w_quantize(part):
-            w_op[part] = operand(ring, "w", LINE * P, 4)
-            spans = ((1, 1), (2, 2)) if part % 2 == 0 else ((0, 4),)
+            w_op[part] = operand(ring, "w", QUAD * P, W_BUFS)
+            spans = ((1, 1), (2, 2)) if first_slot(part) else ((0, QUAD),)
             for first, count in spans:
                 values = w_in[part][:, first * PASS : (first + count) * PASS]
                 quantize(w_op[part], first * P, count * P, values, E4M3)
 
-        late_in, late = {}, {}
+        exp_in, exp_op = {}, {}
 
-        def late_list(step):
-            block, line = divmod(step, 2)
-            if block + 1 == BLOCKS:
-                return []
-            return [(k, block + 1) for k in ((X3,), (EXP, INV))[line]]
-
-        def late_prims(wanted):
-            for k, block in wanted:
-                staged = ring.tile([P, HALVES, PASS], BF16, name="late_in", bufs=4, align_bytes=64)
+        def exp_prims(step):
+            block, quad = divmod(step, 2)
+            for k in EXP_PRIMS[quad]:
+                staged = ring.tile([P, HALVES, PASS], BF16, name="exp_in", bufs=EXP_IN_BUFS, align_bytes=MX_ALIGN)
                 for half in range(HALVES):
-                    from_x = x_int[half][:, block * PASS : (block + 1) * PASS]
-                    from_ln = rows_by_four(ln_x[half][:, :, block * P : (block + 1) * P])
-                    if k == EXP or k == X2:
-                        nc.scalar.activation(out=staged[:, half, :], in_=from_x, func={EXP: ACT.Exp, X2: ACT.Square}[k])
-                    elif k == LN:
-                        nc.scalar.copy(out=interleaved(staged[:, half, :]), in_=from_ln)
+                    if k == EXP:
+                        source = x_int[half][:, block * PASS : (block + 1) * PASS]
+                        nc.scalar.activation(out=staged[:, half, :], in_=source, func=ACT.Exp)
                     else:
-                        scale = {X3: 3.0, INV: -1.0}[k]
-                        nc.scalar.activation(out=interleaved(staged[:, half, :]), in_=from_ln, func=ACT.Exp, scale=scale)
-                late_in[k, block] = staged
+                        nc.scalar.activation(
+                            out=interleaved(staged[:, half, :]),
+                            in_=rows_by_four(ln_x[half][:, :, block * P : (block + 1) * P]),
+                            func=ACT.Exp,
+                            scale={X3: 3.0, INV: -1.0}[k],
+                        )
+                exp_in[k, block] = staged
 
-        def late_quantize(wanted):
-            for k, block in wanted:
-                late[k, block] = operand(ring, "late", HALVES * P, 6)
-                values = late_in[k, block][:].rearrange("p g c -> p (g c)")
-                quantize(late[k, block], 0, HALVES * P, values, E4M3)
+        def exp_quantize(step):
+            block, quad = divmod(step, 2)
+            for k in EXP_PRIMS[quad]:
+                exp_op[k, block] = operand(ring, "exp", HALVES * P, EXP_OPERAND_BUFS)
+                values = exp_in[k, block][:].rearrange("p g c -> p (g c)")
+                quantize(exp_op[k, block], 0, HALVES * P, values, E4M3)
 
         def prim_operand(k, block, half):
-            if (k, half) in whole:
+            if k in WHOLE_PRIMS:
                 (codes, scales), first = whole[k, half], block * P
             else:
-                (codes, scales), first = late[k, block], half * P
+                (codes, scales), first = exp_op[k, block], half * P
             return codes[:, first : first + P].bitcast(E4M3), scales[:, first : first + P]
 
         deriv = {}
 
         def derivs_of_x(step):
             block, half = divmod(step, 2)
-            pair = ring.tile([P, 2, PASS], F32, name="raw_or_deriv", bufs=4)
+            pair = ring.tile([P, 2, PASS], F32, name="raw_or_deriv", bufs=RAW_OR_DERIV_BUFS)
             nc.scalar.activation(out=pair[:, 0, :], in_=x_t[block][:, half, :], func=ACT.Exp)
             nc.scalar.activation(out=pair[:, 1, :], in_=x_t[block][:, half, :], func=ACT.Square)
             deriv[step, X2] = (2.0, x_t[block][:, half, :])
@@ -266,27 +283,24 @@ def tile_dartslayer_v_kernel(tc, x, alphas, coeffs, gates, grad_out, out_0, out_
             deriv[step, EXP] = (1.0, pair[:, 0, :])
             deriv[step, SIN] = (1.0, cos_t[block][:, half, :])
 
-        def ln_transpose(step):
+        def derivs_of_ln(step):
             block, half = divmod(step, 2)
             turned = bank([P, PACK, P])
             for t in range(PACK):
                 nc.tensor.transpose(turned[:, t, :], ln_x[half][:, t, block * P : (block + 1) * P], ident32[:])
-            return turned
-
-        def derivs_of_ln(step, turned):
-            pair = ring.tile([P, 2, PASS], F32, name="raw_or_deriv", bufs=4)
+            pair = ring.tile([P, 2, PASS], F32, name="raw_or_deriv", bufs=RAW_OR_DERIV_BUFS)
             flat = turned[:].rearrange("i t p -> i (t p)")
             nc.scalar.activation(out=pair[:, 0, :], in_=flat, func=ACT.Exp, scale=-1.0)
             nc.scalar.activation(out=pair[:, 1, :], in_=flat, func=ACT.Exp, scale=-2.0)
             deriv[step, LN] = (1.0, pair[:, 0, :])
             deriv[step, INV] = (-1.0, pair[:, 1, :])
 
-        def dprims(step):
+        def dprims_terms(step):
             block, half = divmod(step, 2)
             terms = []
             for k in (X2, X, SIN, EXP, X3, LN, INV):
-                line, slot = divmod(k, LINE)
-                codes, scales = w_op[2 * block + line]
+                quad, slot = divmod(k, QUAD)
+                codes, scales = w_op[2 * block + quad]
                 cols = slice(slot * P, (slot + 1) * P)
                 product = bank([P, PASS])
                 nc.tensor.matmul_mx(
@@ -298,65 +312,54 @@ def tile_dartslayer_v_kernel(tc, x, alphas, coeffs, gates, grad_out, out_0, out_
                     start=True,
                     stop=True,
                 )
+                term = ring.tile([P, PASS], F32, name="term", bufs=PRIMS - 1)
                 if k == X:
-                    term = ring.tile([P, PASS], F32, name="term", bufs=PRIMS - 1)
                     nc.scalar.copy(out=term[:], in_=product[:])
-                    terms.append(term)
                 else:
-                    term = ring.tile([P, PASS], F32, name="term", bufs=PRIMS - 1)
                     factor, values = deriv[step, k]
                     nc.vector.scalar_tensor_tensor(
                         out=term[:], in0=values, scalar=factor, in1=product[:], op0=ALU.mult, op1=ALU.mult
                     )
-                    terms.append(term)
+                terms.append(term)
             return terms
 
-        def sum_terms(terms):
+        def add_turned(total, terms, n, t):
+            nc.tensor.matmul(
+                out=total,
+                lhsT=terms[n][:, t * P : (t + 1) * P],
+                rhs=ident32[:],
+                is_transpose=True,
+                start=(n == 0),
+                stop=(n == len(terms) - 1),
+            )
+
+        def store_dx(step, dx):
+            block, half = divmod(step, 2)
+            nc.sync.dma_start(out=by_token(out_0, half)[:, :, block * P : (block + 1) * P], in_=dx[:])
+
+        def sum_terms(step, terms):
             total = bank([P, PACK, P])
             for t in range(PACK):
-                for n, term in enumerate(terms):
-                    nc.tensor.matmul(
-                        out=total[:, t, :],
-                        lhsT=term[:, t * P : (t + 1) * P],
-                        rhs=ident32[:],
-                        is_transpose=True,
-                        start=(n == 0),
-                        stop=(n == len(terms) - 1),
-                    )
-            return total
-
-        def store_dx(step, total):
-            block, half = divmod(step, 2)
+                for n in range(len(terms)):
+                    add_turned(total[:, t, :], terms, n, t)
             dx = ring.tile([P, PACK, P], F32, name="dx")
             nc.scalar.copy(out=dx[:], in_=total[:])
-            nc.sync.dma_start(out=by_token(out_0, half)[:, :, block * P : (block + 1) * P], in_=dx[:])
+            store_dx(step, dx)
 
-        def finish_dx(step, terms):
-            block, half = divmod(step, 2)
+        def sum_last_terms(step, terms):
             totals = [bank([P, P]) for t in range(PACK)]
-            for n, term in enumerate(terms):
+            for n in range(len(terms)):
                 for t in range(PACK):
-                    nc.tensor.matmul(
-                        out=totals[t][:],
-                        lhsT=term[:, t * P : (t + 1) * P],
-                        rhs=ident32[:],
-                        is_transpose=True,
-                        start=(n == 0),
-                        stop=(n == len(terms) - 1),
-                    )
+                    add_turned(totals[t][:], terms, n, t)
             dx = ring.tile([P, PACK, P], F32, name="dx")
             for t in range(PACK):
-                if t % 2 == 0:
-                    nc.scalar.copy(out=dx[:, t, :], in_=totals[t][:])
-                else:
-                    nc.vector.tensor_copy(out=dx[:, t, :], in_=totals[t][:])
-            nc.sync.dma_start(out=by_token(out_0, half)[:, :, block * P : (block + 1) * P], in_=dx[:])
+                (nc.scalar.copy, nc.vector.tensor_copy)[t % 2](out=dx[:, t, :], in_=totals[t][:])
+            store_dx(step, dx)
 
         def dw_product(step, k):
-            block = step // 2
             product = bank([P, OUT])
             for half in range(HALVES):
-                codes, scales = prim_operand(k, block, half)
+                codes, scales = prim_operand(k, step // 2, half)
                 nc.tensor.matmul_mx(
                     out=product[:],
                     lhsT=codes,
@@ -368,87 +371,98 @@ def tile_dartslayer_v_kernel(tc, x, alphas, coeffs, gates, grad_out, out_0, out_
                 )
             return product
 
+        def held_outs(step):
+            return HELD_OUTS if step + W_AHEAD < STEPS else OUT
+
         def dw_products(step):
-            line = step % 2
-            for k in EARLY_DW[line]:
-                nc.scalar.copy(out=dw[line][:, k % LINE, :], in_=dw_product(step, k)[:])
-            return dw_product(step, LAST_DW[line])
+            quad = step % 2
+            for k in EARLY_DW[quad]:
+                nc.scalar.copy(out=dw[quad][:, k % QUAD, :], in_=dw_product(step, k)[:])
+            product = dw_product(step, LAST_DW[quad])
+            if held_outs(step) < OUT:
+                rest = slice(held_outs(step), OUT)
+                nc.scalar.copy(out=dw[quad][:, LAST_DW[quad] % QUAD, rest], in_=product[:, rest])
+            return product
 
-        def dw_last_copy(step, product, outs):
-            line = step % 2
-            nc.vector.tensor_copy(out=dw[line][:, LAST_DW[line] % LINE, outs], in_=product[:, outs])
+        def copy_held(step, product, outs):
+            quad = step % 2
+            nc.vector.tensor_copy(out=dw[quad][:, LAST_DW[quad] % QUAD, outs], in_=product[:, outs])
 
-        def store_dw(step, outs):
-            block, line = divmod(step, 2)
-            if line == 1:
+        def store_dcoeffs(step, outs):
+            block, quad = divmod(step, 2)
+            if quad == 1:
                 rows = out_1[block * P : (block + 1) * P, :, :].rearrange("i j k -> i (j k)")
                 cols = slice(outs.start * PRIMS, outs.stop * PRIMS)
                 nc.sync.dma_start(out=rows[:, cols], in_=gate[block][:, cols])
 
         def dw_multiply_gpsimd(step):
-            block, line = divmod(step, 2)
-            gate_view = gate[block][:].rearrange("i (j l k) -> i j l k", l=2, k=LINE)
-            dw_view = dw[line][:].rearrange("i k j -> i j k")
+            block, quad = divmod(step, 2)
+            gate_view = gate[block][:].rearrange("i (j q k) -> i j q k", q=2, k=QUAD)
+            dw_view = dw[quad][:].rearrange("i k j -> i j k")
             for first in range(0, GPSIMD_OUTS, GPSIMD_OUTS // 2):
                 outs = slice(first, first + GPSIMD_OUTS // 2)
-                target = gate_view[:, outs, line, :]
+                target = gate_view[:, outs, quad, :]
                 nc.gpsimd.tensor_tensor(out=target, in0=dw_view[:, outs, :], in1=target, op=ALU.mult)
-                store_dw(step, outs)
+                store_dcoeffs(step, outs)
 
         def dw_multiply_vector(step):
-            block, line = divmod(step, 2)
-            gate_view = gate[block][:].rearrange("i (c e l k) -> i c l k e", e=2, l=2, k=LINE)
-            dw_view = dw[line][:].rearrange("i k (c e) -> i c k e", e=2)
+            block, quad = divmod(step, 2)
+            gate_view = gate[block][:].rearrange("i (c e q k) -> i c q k e", e=2, q=2, k=QUAD)
+            dw_view = dw[quad][:].rearrange("i k (c e) -> i c k e", e=2)
             pairs = slice(GPSIMD_OUTS // 2, OUT // 2)
-            target = gate_view[:, pairs, line, :, :]
+            target = gate_view[:, pairs, quad, :, :]
             nc.vector.tensor_tensor(out=target, in0=dw_view[:, pairs, :, :], in1=target, op=ALU.mult)
-            store_dw(step, slice(GPSIMD_OUTS, OUT))
-            if line == 1 and block + 3 < BLOCKS:
-                load_gates(block + 3)
+            store_dcoeffs(step, slice(GPSIMD_OUTS, OUT))
+            if quad == 1 and block + GATE_BUFS < BLOCKS:
+                load_gates(block + GATE_BUFS)
 
+        w_multiply(0)
+        w_multiply(1)
+        cosines(range(0, BLOCKS // 2))
+        w_transpose(0)
+        cosines(range(BLOCKS // 2, BLOCKS))
+        w_transpose(1)
+        finish_whole_prims()
         dw = [
-            shared.tile([P, LINE, OUT], F32, name="dw%d" % line, offset=line * LINE * OUT * 4, align_bytes=64)
-            for line in range(2)
+            shared.tile([P, QUAD, OUT], F32, name="dw%d" % quad, offset=quad * QUAD * OUT * 4, align_bytes=MX_ALIGN)
+            for quad in range(2)
         ]
         nc.gpsimd.memset(dw[0][:, 0, :], 0.0)
-        w_multiply(0)
-        w_copy(w_transpose(0))
-        w_multiply(1)
-        for half in range(HALVES):
-            quantize(whole[SIN, half], 0, PASS, sin_in[half][:], E4M3)
-        w_copy(w_transpose(1))
-        late_prims(late_list(-2))
+        exp_prims(0)
         w_quantize(0)
-        w_multiply(2)
         w_quantize(1)
-        late_quantize(late_list(-2))
-        held = dw_products(0)
         derivs_of_x(0)
-        derivs_of_ln(0, ln_transpose(0))
-        late_prims(late_list(-1))
+        derivs_of_ln(0)
+        exp_quantize(0)
+        held = dw_products(0)
+        w_multiply(2)
+        exp_prims(1)
 
         for step in range(STEPS - 1):
-            dw_last_copy(step, held, slice(0, OUT))
+            copy_held(step, held, slice(0, held_outs(step)))
             dw_multiply_gpsimd(step)
-            terms = dprims(step)
+            terms = dprims_terms(step)
             if step == 0:
-                late_quantize(late_list(-1))
+                exp_quantize(1)
             dw_multiply_vector(step)
-            late_prims(late_list(step))
+            if step + 2 < STEPS:
+                exp_prims(step + 2)
             derivs_of_x(step + 1)
             held = dw_products(step + 1)
-            derivs_of_ln(step + 1, ln_transpose(step + 1))
+            derivs_of_ln(step + 1)
+            if step + W_AHEAD - 1 < STEPS:
+                w_transpose(step + W_AHEAD - 1)
+            sum_terms(step, terms)
             if step + 2 < STEPS:
-                w_copy(w_transpose(step + 2))
-            store_dx(step, sum_terms(terms))
-            late_quantize(late_list(step))
-            if step + 3 < STEPS:
-                w_multiply(step + 3)
-            if step + 2 < STEPS:
-                w_quantize(step + 2)
-        step = STEPS - 1
-        dw_last_copy(step, held, slice(GPSIMD_OUTS, OUT))
-        dw_multiply_vector(step)
-        dw_last_copy(step, held, slice(0, GPSIMD_OUTS))
-        dw_multiply_gpsimd(step)
-        finish_dx(step, dprims(step))
+                exp_quantize(step + 2)
+            if step + W_AHEAD < STEPS:
+                w_multiply(step + W_AHEAD)
+            if step + W_AHEAD - 1 < STEPS:
+                w_quantize(step + W_AHEAD - 1)
+
+        last = STEPS - 1
+        copy_held(last, held, slice(GPSIMD_OUTS, OUT))
+        dw_multiply_vector(last)
+        copy_held(last, held, slice(0, GPSIMD_OUTS))
+        dw_multiply_gpsimd(last)
+        sum_last_terms(last, dprims_terms(last))

import math
from contextlib import ExitStack

import concourse.mybir as mybir
from concourse.masks import make_identity

F32 = mybir.dt.float32
BF16 = mybir.dt.bfloat16
U32 = mybir.dt.uint32
U8 = mybir.dt.uint8
E4M3 = mybir.dt.float8_e4m3fn_x4
E5M2 = mybir.dt.float8_e5m2_x4
ACT = mybir.ActivationFunctionType
ALU = mybir.AluOpType

TOKENS, IN, OUT, PRIMS = 1024, 512, 512, 8
FLOPS = 2 * 2 * TOKENS * IN * OUT * (PRIMS - 1)
BYTES = TOKENS * IN * 2 + IN * OUT * PRIMS * (2 + 4 + 4) + TOKENS * OUT * 2 + TOKENS * IN * 4

P = 128
PACK = 4
PASS = P * PACK
HALVES = TOKENS // PASS
BLOCKS = IN // P
QUAD = 4
STEPS = BLOCKS * 2
MX_ALIGN = 64
X, X2, X3, EXP, LN, INV, SIN = 1, 2, 3, 4, 5, 6, 7

WHOLE_PRIMS = (X, X2, LN, SIN)
EXP_PRIMS = ((X3,), (EXP, INV))
EARLY_DW = ((X, X2), (LN, SIN, EXP))
LAST_DW = (X3, INV)

GPSIMD_OUTS = 256
HELD_OUTS = 64
W_AHEAD = 3

GATE_BUFS = 3
RAW_OR_DERIV_BUFS = 4
W_BUFS = 4
EXP_IN_BUFS = 4
EXP_OPERAND_BUFS = 6


def tile_dartslayer_v_kernel(tc, x, alphas, coeffs, gates, grad_out, out_0, out_1):
    nc = tc.nc
    with ExitStack() as ctx:
        keep = ctx.enter_context(tc.tile_pool(name="keep", bufs=1))
        ring = ctx.enter_context(tc.tile_pool(name="ring", bufs=2))
        shared = ctx.enter_context(tc.tile_pool(name="shared", bufs=1))
        psum = ctx.enter_context(tc.psum_pool(name="psum", bufs=8))
        ctx.enter_context(tc.manual_schedule())

        def bank(shape, dtype=F32):
            return psum.tile(shape, dtype, name="bank")

        def operand(pool, name, width, bufs):
            codes = pool.tile([P, width], U32, name=name + "_codes", bufs=bufs, align_bytes=MX_ALIGN)
            scales = pool.tile([P, width], U8, name=name + "_scales", bufs=bufs, align_bytes=MX_ALIGN)
            return codes, scales

        def quantize(target, first, count, values, fmt):
            codes, scales = target
            cols = slice(first, first + count)
            nc.vector.quantize_mx(out=codes[:, cols].bitcast(fmt), scales=scales[:, cols], in_=values)

        def by_token(tensor, half):
            return tensor[half * PASS : (half + 1) * PASS, :].rearrange("(p t) w -> p t w", t=PACK)

        x_raw, g_raw = [], []
        for source, tiles in ((x, x_raw), (grad_out, g_raw)):
            for half in range(HALVES):
                raw = ring.tile([P, PACK, IN], BF16, name="raw_or_deriv", bufs=RAW_OR_DERIV_BUFS)
                nc.sync.dma_start(out=raw[:], in_=by_token(source, half))
                tiles.append(raw)

        gate, coeff = {}, {}

        def load_gates(block):
            gate[block] = ring.tile([P, OUT * PRIMS], F32, name="gate", bufs=GATE_BUFS)
            rows = gates[block * P : (block + 1) * P, :, :]
            nc.sync.dma_start(out=gate[block][:], in_=rows.rearrange("i j k -> i (j k)"))

        def load_coeffs(block):
            coeff[block] = ring.tile([P, OUT * PRIMS], BF16, name="coeff")
            rows = coeffs[block * P : (block + 1) * P, :, :]
            nc.sync.dma_start(out=coeff[block][:], in_=rows.rearrange("i j k -> i (j k)"))

        for block in range(2):
            load_gates(block)
            load_coeffs(block)
        load_gates(2)

        ident32 = keep.tile([P, P], F32)
        ident16 = keep.tile([P, P], BF16)
        make_identity(nc, ident16[:])
        make_identity(nc, ident32[:])

        def stage(ring_index):
            offset = ring_index * 2 * PASS * PACK * 2
            name = "stage%d" % ring_index
            return shared.tile([P, PASS * PACK], BF16, name=name, bufs=2, offset=offset, align_bytes=MX_ALIGN)

        def interleaved(flat):
            return flat.rearrange("p (c n t) -> p c t n", n=4, t=PACK)

        def rows_by_four(rows):
            return rows.rearrange("p t (c n) -> p c t n", n=4)

        x_int = [keep.tile([P, IN * PACK], BF16, name="x_int%d" % h, align_bytes=MX_ALIGN) for h in range(HALVES)]
        ln_x = [keep.tile([P, PACK, IN], F32, name="ln_x%d" % h) for h in range(HALVES)]
        x_t = [keep.tile([P, HALVES, PASS], BF16, name="x_t%d" % b) for b in range(BLOCKS)]
        cos_t = [keep.tile([P, HALVES, PASS], F32, name="cos_t%d" % b) for b in range(BLOCKS)]
        whole = {(k, h): operand(keep, "prim%d_%d" % (k, h), IN, 1) for k in WHOLE_PRIMS for h in range(HALVES)}
        g_tok = [operand(keep, "g_tok%d" % h, OUT, 1) for h in range(HALVES)]
        g_feat = [operand(keep, "g_feat%d" % h, PASS, 1) for h in range(HALVES)]

        for half in range(HALVES):
            nc.scalar.activation(out=ln_x[half][:], in_=x_raw[half][:], func=ACT.Ln)
            nc.vector.tensor_copy(out=interleaved(x_int[half][:]), in_=rows_by_four(x_raw[half][:]))

        for half in range(HALVES):
            for block in range(BLOCKS):
                turned = bank([P, PACK, P], BF16)
                for t in range(PACK):
                    nc.tensor.transpose(turned[:, t, :], x_raw[half][:, t, block * P : (block + 1) * P], ident16[:])
                nc.scalar.copy(out=x_t[block][:, half, :], in_=turned[:].rearrange("i t p -> i (t p)"))

        def g_transpose(half):
            staged = stage(1)
            staged_words = staged[:].bitcast(F32).rearrange("p (t r u) -> p t r u", t=PACK, u=2)
            g_words = g_raw[half][:].rearrange("p t j -> p (t j)").bitcast(F32)
            copies = []
            for slot_pair in range(PACK // 2):
                turned = bank([P, 2, 2, P])
                for tt in range(2):
                    first = (2 * slot_pair + tt) * (OUT // 2)
                    for u in range(2):
                        nc.tensor.transpose(turned[:, tt, u, :], g_words[:, first + u : first + OUT // 2 : 2], ident32[:])
                target = staged_words[:, 2 * slot_pair : 2 * slot_pair + 2, :, :]
                copies.append((target, turned[:].rearrange("p t u r -> p t r u")))
            return staged, copies

        def copy_all(copy, copies):
            for target, source in copies:
                copy(out=target, in_=source)

        g_feat_in, g_copies = zip(*[g_transpose(half) for half in range(HALVES)])
        copy_all(nc.scalar.copy, g_copies[0])

        def interleave(rows):
            staged = stage(0)
            nc.vector.tensor_copy(out=interleaved(staged[:]), in_=rows_by_four(rows))
            return staged

        g_tok_in = []
        for half in range(HALVES):
            quantize(whole[X, half], 0, IN, x_int[half][:], E4M3)
            g_tok_in.append(interleave(g_raw[half][:]))
        copy_all(nc.vector.tensor_copy, g_copies[1])
        for half in range(HALVES):
            quantize(g_tok[half], 0, OUT, g_tok_in[half][:], E5M2)
            quantize(g_feat[half], 0, PASS, g_feat_in[half][:], E5M2)

        sin_in = []
        for half in range(HALVES):
            staged = stage(1)
            nc.scalar.activation(out=staged[:], in_=x_int[half][:], func=ACT.Sin)
            sin_in.append(staged)

        def cosines(blocks):
            for block in blocks:
                nc.scalar.activation(out=cos_t[block][:], in_=x_t[block][:], func=ACT.Sin, scale=-1.0, bias=math.pi / 2)

        def finish_whole_prims():
            squares, logs = [], []
            for half in range(HALVES):
                staged = stage(0)
                nc.vector.tensor_tensor(out=staged[:], in0=x_int[half][:], in1=x_int[half][:], op=ALU.mult)
                squares.append(staged)
            for half in range(HALVES):
                quantize(whole[X2, half], 0, IN, squares[half][:], E4M3)
                logs.append(interleave(ln_x[half][:]))
            for half in range(HALVES):
                quantize(whole[SIN, half], 0, IN, sin_in[half][:], E4M3)
                quantize(whole[LN, half], 0, IN, logs[half][:], E4M3)

        w_rows, w_in, w_op = {}, {}, {}

        def first_slot(part):
            return 1 if part % 2 == 0 else 0

        def w_multiply(part):
            block, quad = divmod(part, 2)
            w_rows[part] = ring.tile([P, QUAD, 2, P, 2], BF16, name="w_rows")
            gate_view = gate[block][:].rearrange("i (p u e k) -> i u p e k", u=2, e=2, k=PRIMS)
            coeff_view = coeff[block][:].rearrange("i (p u e k) -> i u p e k", u=2, e=2, k=PRIMS)
            if quad == 0:
                nc.vector.tensor_tensor(
                    out=w_rows[part][:, X, :, :, :],
                    in0=gate_view[:, :, :, :, X],
                    in1=coeff_view[:, :, :, :, X],
                    op=ALU.mult,
                )
            for slot in range(2 * first_slot(part), QUAD, 2):
                ks = slice(QUAD * quad + slot, QUAD * quad + slot + 2)
                for u in range(2):
                    nc.vector.tensor_tensor(
                        out=w_rows[part][:, slot : slot + 2, u, :, :].rearrange("i k p e -> i p e k"),
                        in0=gate_view[:, u, :, :, ks],
                        in1=coeff_view[:, u, :, :, ks],
                        op=ALU.mult,
                    )
            if quad == 1 and block + 2 < BLOCKS:
                load_coeffs(block + 2)

        def w_transpose(part):
            w_in[part] = ring.tile([P, QUAD * P * PACK], BF16, name="w_in", align_bytes=MX_ALIGN)
            in_words = w_in[part][:].bitcast(F32).rearrange("p (k i u) -> p k i u", k=QUAD, u=2)
            row_words = w_rows[part][:].rearrange("i k u p e -> i (k u p e)").bitcast(F32)
            copies = []
            for slot in range(0, QUAD, 2):
                turned = bank([P, 2, 2, P])
                skip = max(first_slot(part) - slot, 0)
                for kk in range(skip, 2):
                    for u in range(2):
                        first = ((slot + kk) * 2 + u) * P
                        nc.tensor.transpose(turned[:, kk, u, :], row_words[:, first : first + P], ident32[:])
                source = turned[:, skip:2, :, :].rearrange("p k u i -> p k i u")
                copies.append((in_words[:, slot + skip : slot + 2, :, :], source))
            copy_all(nc.scalar.copy, copies)

        def w_quantize(part):
            w_op[part] = operand(ring, "w", QUAD * P, W_BUFS)
            spans = ((1, 1), (2, 2)) if first_slot(part) else ((0, QUAD),)
            for first, count in spans:
                values = w_in[part][:, first * PASS : (first + count) * PASS]
                quantize(w_op[part], first * P, count * P, values, E4M3)

        exp_in, exp_op = {}, {}

        def exp_prims(step):
            block, quad = divmod(step, 2)
            for k in EXP_PRIMS[quad]:
                staged = ring.tile([P, HALVES, PASS], BF16, name="exp_in", bufs=EXP_IN_BUFS, align_bytes=MX_ALIGN)
                for half in range(HALVES):
                    if k == EXP:
                        source = x_int[half][:, block * PASS : (block + 1) * PASS]
                        nc.scalar.activation(out=staged[:, half, :], in_=source, func=ACT.Exp)
                    else:
                        nc.scalar.activation(
                            out=interleaved(staged[:, half, :]),
                            in_=rows_by_four(ln_x[half][:, :, block * P : (block + 1) * P]),
                            func=ACT.Exp,
                            scale={X3: 3.0, INV: -1.0}[k],
                        )
                exp_in[k, block] = staged

        def exp_quantize(step):
            block, quad = divmod(step, 2)
            for k in EXP_PRIMS[quad]:
                exp_op[k, block] = operand(ring, "exp", HALVES * P, EXP_OPERAND_BUFS)
                values = exp_in[k, block][:].rearrange("p g c -> p (g c)")
                quantize(exp_op[k, block], 0, HALVES * P, values, E4M3)

        def prim_operand(k, block, half):
            if k in WHOLE_PRIMS:
                (codes, scales), first = whole[k, half], block * P
            else:
                (codes, scales), first = exp_op[k, block], half * P
            return codes[:, first : first + P].bitcast(E4M3), scales[:, first : first + P]

        deriv = {}

        def derivs_of_x(step):
            block, half = divmod(step, 2)
            pair = ring.tile([P, 2, PASS], F32, name="raw_or_deriv", bufs=RAW_OR_DERIV_BUFS)
            nc.scalar.activation(out=pair[:, 0, :], in_=x_t[block][:, half, :], func=ACT.Exp)
            nc.scalar.activation(out=pair[:, 1, :], in_=x_t[block][:, half, :], func=ACT.Square)
            deriv[step, X2] = (2.0, x_t[block][:, half, :])
            deriv[step, X3] = (3.0, pair[:, 1, :])
            deriv[step, EXP] = (1.0, pair[:, 0, :])
            deriv[step, SIN] = (1.0, cos_t[block][:, half, :])

        def derivs_of_ln(step):
            block, half = divmod(step, 2)
            turned = bank([P, PACK, P])
            for t in range(PACK):
                nc.tensor.transpose(turned[:, t, :], ln_x[half][:, t, block * P : (block + 1) * P], ident32[:])
            pair = ring.tile([P, 2, PASS], F32, name="raw_or_deriv", bufs=RAW_OR_DERIV_BUFS)
            flat = turned[:].rearrange("i t p -> i (t p)")
            nc.scalar.activation(out=pair[:, 0, :], in_=flat, func=ACT.Exp, scale=-1.0)
            nc.scalar.activation(out=pair[:, 1, :], in_=flat, func=ACT.Exp, scale=-2.0)
            deriv[step, LN] = (1.0, pair[:, 0, :])
            deriv[step, INV] = (-1.0, pair[:, 1, :])

        def dprims_terms(step):
            block, half = divmod(step, 2)
            terms = []
            for k in (X2, X, SIN, EXP, X3, LN, INV):
                quad, slot = divmod(k, QUAD)
                codes, scales = w_op[2 * block + quad]
                cols = slice(slot * P, (slot + 1) * P)
                product = bank([P, PASS])
                nc.tensor.matmul_mx(
                    out=product[:],
                    lhsT=codes[:, cols].bitcast(E4M3),
                    lhsT_scale=scales[:, cols],
                    rhs=g_feat[half][0][:].bitcast(E5M2),
                    rhs_scale=g_feat[half][1][:],
                    start=True,
                    stop=True,
                )
                term = ring.tile([P, PASS], F32, name="term", bufs=PRIMS - 1)
                if k == X:
                    nc.scalar.copy(out=term[:], in_=product[:])
                else:
                    factor, values = deriv[step, k]
                    nc.vector.scalar_tensor_tensor(
                        out=term[:], in0=values, scalar=factor, in1=product[:], op0=ALU.mult, op1=ALU.mult
                    )
                terms.append(term)
            return terms

        def add_turned(total, terms, n, t):
            nc.tensor.matmul(
                out=total,
                lhsT=terms[n][:, t * P : (t + 1) * P],
                rhs=ident32[:],
                is_transpose=True,
                start=(n == 0),
                stop=(n == len(terms) - 1),
            )

        def store_dx(step, dx):
            block, half = divmod(step, 2)
            nc.sync.dma_start(out=by_token(out_0, half)[:, :, block * P : (block + 1) * P], in_=dx[:])

        def sum_terms(step, terms):
            total = bank([P, PACK, P])
            for t in range(PACK):
                for n in range(len(terms)):
                    add_turned(total[:, t, :], terms, n, t)
            dx = ring.tile([P, PACK, P], F32, name="dx")
            nc.scalar.copy(out=dx[:], in_=total[:])
            store_dx(step, dx)

        def sum_last_terms(step, terms):
            totals = [bank([P, P]) for t in range(PACK)]
            for n in range(len(terms)):
                for t in range(PACK):
                    add_turned(totals[t][:], terms, n, t)
            dx = ring.tile([P, PACK, P], F32, name="dx")
            for t in range(PACK):
                (nc.scalar.copy, nc.vector.tensor_copy)[t % 2](out=dx[:, t, :], in_=totals[t][:])
            store_dx(step, dx)

        def dw_product(step, k):
            product = bank([P, OUT])
            for half in range(HALVES):
                codes, scales = prim_operand(k, step // 2, half)
                nc.tensor.matmul_mx(
                    out=product[:],
                    lhsT=codes,
                    lhsT_scale=scales,
                    rhs=g_tok[half][0][:].bitcast(E5M2),
                    rhs_scale=g_tok[half][1][:],
                    start=(half == 0),
                    stop=(half == HALVES - 1),
                )
            return product

        def held_outs(step):
            return HELD_OUTS if step + W_AHEAD < STEPS else OUT

        def dw_products(step):
            quad = step % 2
            for k in EARLY_DW[quad]:
                nc.scalar.copy(out=dw[quad][:, k % QUAD, :], in_=dw_product(step, k)[:])
            product = dw_product(step, LAST_DW[quad])
            if held_outs(step) < OUT:
                rest = slice(held_outs(step), OUT)
                nc.scalar.copy(out=dw[quad][:, LAST_DW[quad] % QUAD, rest], in_=product[:, rest])
            return product

        def copy_held(step, product, outs):
            quad = step % 2
            nc.vector.tensor_copy(out=dw[quad][:, LAST_DW[quad] % QUAD, outs], in_=product[:, outs])

        def store_dcoeffs(step, outs):
            block, quad = divmod(step, 2)
            if quad == 1:
                rows = out_1[block * P : (block + 1) * P, :, :].rearrange("i j k -> i (j k)")
                cols = slice(outs.start * PRIMS, outs.stop * PRIMS)
                nc.sync.dma_start(out=rows[:, cols], in_=gate[block][:, cols])

        def dw_multiply_gpsimd(step):
            block, quad = divmod(step, 2)
            gate_view = gate[block][:].rearrange("i (j q k) -> i j q k", q=2, k=QUAD)
            dw_view = dw[quad][:].rearrange("i k j -> i j k")
            for first in range(0, GPSIMD_OUTS, GPSIMD_OUTS // 2):
                outs = slice(first, first + GPSIMD_OUTS // 2)
                target = gate_view[:, outs, quad, :]
                nc.gpsimd.tensor_tensor(out=target, in0=dw_view[:, outs, :], in1=target, op=ALU.mult)
                store_dcoeffs(step, outs)

        def dw_multiply_vector(step):
            block, quad = divmod(step, 2)
            gate_view = gate[block][:].rearrange("i (c e q k) -> i c q k e", e=2, q=2, k=QUAD)
            dw_view = dw[quad][:].rearrange("i k (c e) -> i c k e", e=2)
            pairs = slice(GPSIMD_OUTS // 2, OUT // 2)
            target = gate_view[:, pairs, quad, :, :]
            nc.vector.tensor_tensor(out=target, in0=dw_view[:, pairs, :, :], in1=target, op=ALU.mult)
            store_dcoeffs(step, slice(GPSIMD_OUTS, OUT))
            if quad == 1 and block + GATE_BUFS < BLOCKS:
                load_gates(block + GATE_BUFS)

        w_multiply(0)
        w_multiply(1)
        cosines(range(0, BLOCKS // 2))
        w_transpose(0)
        cosines(range(BLOCKS // 2, BLOCKS))
        w_transpose(1)
        finish_whole_prims()
        dw = [
            shared.tile([P, QUAD, OUT], F32, name="dw%d" % quad, offset=quad * QUAD * OUT * 4, align_bytes=MX_ALIGN)
            for quad in range(2)
        ]
        nc.gpsimd.memset(dw[0][:, 0, :], 0.0)
        exp_prims(0)
        w_quantize(0)
        w_quantize(1)
        derivs_of_x(0)
        derivs_of_ln(0)
        exp_quantize(0)
        held = dw_products(0)
        w_multiply(2)
        exp_prims(1)

        for step in range(STEPS - 1):
            copy_held(step, held, slice(0, held_outs(step)))
            dw_multiply_gpsimd(step)
            terms = dprims_terms(step)
            if step == 0:
                exp_quantize(1)
            dw_multiply_vector(step)
            if step + 2 < STEPS:
                exp_prims(step + 2)
            derivs_of_x(step + 1)
            held = dw_products(step + 1)
            derivs_of_ln(step + 1)
            if step + W_AHEAD - 1 < STEPS:
                w_transpose(step + W_AHEAD - 1)
            sum_terms(step, terms)
            if step + 2 < STEPS:
                exp_quantize(step + 2)
            if step + W_AHEAD < STEPS:
                w_multiply(step + W_AHEAD)
            if step + W_AHEAD - 1 < STEPS:
                w_quantize(step + W_AHEAD - 1)

        last = STEPS - 1
        copy_held(last, held, slice(GPSIMD_OUTS, OUT))
        dw_multiply_vector(last)
        copy_held(last, held, slice(0, GPSIMD_OUTS))
        dw_multiply_gpsimd(last)
        sum_last_terms(last, dprims_terms(last))
